import numpy as np
import ml_dtypes


def mxq(x, axis, fmt="e4m3"):
    dtype, down = {"e4m3": (ml_dtypes.float8_e4m3fn, 7), "e5m2": (ml_dtypes.float8_e5m2, 14)}[fmt]
    v = np.moveaxis(np.asarray(x, np.float32).astype(ml_dtypes.bfloat16).astype(np.float64), axis, -1)
    blocks = v.reshape(v.shape[:-1] + (-1, 32))
    amax = np.abs(blocks).max(-1, keepdims=True)
    byte = np.maximum(np.where(amax > 0, np.frexp(amax)[1] - 1 + 127, 0) - down, 1)
    scale = np.exp2(byte - 127.0)
    codes = (blocks / scale).astype(np.float32).astype(dtype).astype(np.float64)
    return np.moveaxis((codes * scale).reshape(v.shape), -1, axis)


WIDE = False


def mx_kscale(k):
    if not WIDE:
        return np.ones(k)
    levels = np.array([10, -10, 5, -5, 0])
    a = np.random.permutation(np.resize(levels, k // 512 * 4)).reshape(k // 512, 4)
    idx = np.arange(k)
    return np.exp2(a[idx // 512, idx % 128 // 32])


BF16 = ml_dtypes.bfloat16


def bf(x):
    return np.asarray(x, np.float32).astype(BF16)


def f64(x):
    return np.asarray(x).astype(np.float64)


E2M1 = np.array([0.0, 0.5, 1.0, 1.5, 2.0, 3.0, 4.0, 6.0, -0.0, -0.5, -1.0, -1.5, -2.0, -3.0, -4.0, -6.0])


def pack_weight(w, fmt):
    k, n = w.shape
    w = f64(bf(w)).reshape(k // 32, 32, n)
    amax = np.abs(w).max(1)
    if fmt == "e4m3":
        byte = np.frexp(amax)[1] - 1 + 127 - 7
    else:
        mant, ex = np.frexp(amax / 6.0)
        byte = np.where(mant > 0.5, ex, ex - 1) + 127
    byte = np.clip(np.where(amax > 0, byte, 1), 1, 254)
    scaled = (w * np.exp2(127.0 - byte)[:, None, :]).reshape(k, n).astype(np.float32)
    by_word = np.ascontiguousarray(scaled.reshape(k // 512, 128, 4, n).transpose(0, 1, 3, 2))
    if fmt == "e4m3":
        words = by_word.astype(ml_dtypes.float8_e4m3fn).view(np.uint8)
    else:
        c = by_word.astype(ml_dtypes.float4_e2m1fn).view(np.uint8) & 0xF
        words = c[..., 0::2] | (c[..., 1::2] << 4)
    return np.ascontiguousarray(words), np.ascontiguousarray(byte.astype(np.uint8).reshape(k // 512, 16, n))


def unpack_weight(words, scales, fmt):
    g, p, n, _ = words.shape
    if fmt == "e4m3":
        vals = np.ascontiguousarray(words).view(ml_dtypes.float8_e4m3fn).astype(np.float64)
    else:
        nib = np.empty((g, p, n, 4), np.uint8)
        nib[..., 0::2] = words & 0xF
        nib[..., 1::2] = words >> 4
        vals = E2M1[nib]
    vals = vals * np.repeat(np.exp2(scales.astype(np.float64) - 127.0), 8, axis=1)[..., None]
    return vals.transpose(0, 1, 3, 2).reshape(g * 512, n)


M, D, F = 256, 1024, 4096


def silu(v):
    return v / (1.0 + np.exp(-v))


def setup_inputs():
    s, t = mx_kscale(D), mx_kscale(F)
    x = bf(np.random.standard_normal((M, D)) * s)
    w_gate = np.random.standard_normal((D, F)) * 0.04 / s[:, None]
    w_up = np.random.standard_normal((D, F)) * 0.04 / s[:, None] * t
    w_down = np.random.standard_normal((F, D)) * 0.03 / t[:, None]
    gate_words, gate_scales = pack_weight(w_gate, "e4m3")
    up_words, up_scales = pack_weight(w_up, "e4m3")
    down_words, down_scales = pack_weight(w_down, "e4m3")
    return {"x": x, "gate_words": gate_words, "gate_scales": gate_scales, "up_words": up_words, "up_scales": up_scales,
            "down_words": down_words, "down_scales": down_scales}


def reference(x, gate_words, gate_scales, up_words, up_scales, down_words, down_scales):
    w_gate = unpack_weight(gate_words, gate_scales, "e4m3")
    w_up = unpack_weight(up_words, up_scales, "e4m3")
    w_down = unpack_weight(down_words, down_scales, "e4m3")
    xq = mxq(f64(x), 1, "e4m3")
    g = xq @ w_gate
    u = xq @ w_up
    h = silu(g) * u
    return mxq(h, 1, "e4m3") @ w_down

@@ -1,0 +1,261 @@
+from contextlib import ExitStack
+
+import concourse.mybir as mybir
+from concourse.masks import make_identity
+
+FP8X4 = mybir.dt.float8_e4m3fn_x4
+BF16 = mybir.dt.bfloat16
+F32 = mybir.dt.float32
+I32 = mybir.dt.int32
+U32 = mybir.dt.uint32
+U8 = mybir.dt.uint8
+
+P = 128
+M, D, F = 256, 1024, 4096
+M_TILES = M // P
+K_PASS = 512
+D_GROUPS = D // K_PASS
+F_GROUPS = F // K_PASS
+N_TILE = 512
+N_HALVES = D // N_TILE
+
+FLOPS = 2 * M * D * F * 3
+
+LOAD_COLS = ((0, 512), (512, 1024), (1024, 2048), (2048, 3072), (3072, 4096))
+
+
+def tile_mlp_kernel(
+    tc, x, gate_words, gate_scales, up_words, up_scales, down_words, down_scales, out
+):
+    nc = tc.nc
+    silu = mybir.ActivationFunctionType.Silu
+    mult = mybir.AluOpType.mult
+
+    with ExitStack() as ctx:
+        keep = ctx.enter_context(tc.tile_pool(name="keep", bufs=1))
+        work = ctx.enter_context(tc.tile_pool(name="work", bufs=1))
+        psum = ctx.enter_context(tc.psum_pool(name="psum", bufs=1))
+        ctx.enter_context(tc.manual_schedule())
+
+        warm_in = keep.tile([P, 8], F32)
+        warm_out = keep.tile([P, 8], F32)
+        nc.vector.memset(warm_in[:], 0.0)
+        nc.scalar.activation(out=warm_out[:], in_=warm_in[:], func=silu)
+
+        gate_planes = keep.tile([P, F], U8, align_bytes=64)
+        up_planes = keep.tile([P, F], U8, align_bytes=64)
+        down_planes = keep.tile([P, 2, D], U8, align_bytes=64)
+        nc.vector.memset(gate_planes[:].bitcast(I32), 0)
+        nc.vector.memset(up_planes[:].bitcast(I32), 0)
+        nc.vector.memset(down_planes[:].rearrange("p a n -> p (a n)").bitcast(I32), 0)
+
+        ident_f = keep.tile([P, P], F32)
+        make_identity(nc, ident_f[:])
+        ident_b = keep.tile([P, P], BF16)
+        make_identity(nc, ident_b[:])
+
+        x_sb = []
+        for mt in range(M_TILES):
+            x_t = keep.tile([P, D], BF16, name="x_sb%d" % mt)
+            nc.sync.dma_start(out=x_t[:], in_=x[mt * P : (mt + 1) * P, :])
+            x_sb.append(x_t)
+
+        def load_planes(planes, scales, first):
+            for q in range(4):
+                nc.sync.dma_start(
+                    out=planes[32 * q + first : 32 * q + first + 8, :].bitcast(I32),
+                    in_=scales[:, 4 * q : 4 * q + 4, :].bitcast(I32),
+                )
+
+        gate_view = gate_words.rearrange("g p n t -> p g (n t)")
+        up_view = up_words.rearrange("g p n t -> p g (n t)")
+        down_view = down_words.rearrange("g p n t -> p g (n t)")
+
+        def load_words(view, lo, hi, name):
+            w_t = keep.tile([P, D_GROUPS, hi - lo], U32, name=name, align_bytes=64)
+            nc.sync.dma_start(
+                out=w_t[:].bitcast(I32), in_=view[:, :, 4 * lo : 4 * hi].bitcast(I32)
+            )
+            return w_t
+
+        gate_sb = []
+        up_sb = []
+        for i, (lo, hi) in enumerate(LOAD_COLS):
+            if i == 0:
+                load_planes(gate_planes, gate_scales, 0)
+            gate_sb.append(load_words(gate_view, lo, hi, "gate_sb%d" % i))
+            if i == 0:
+                load_planes(up_planes, up_scales, 8)
+            up_sb.append(load_words(up_view, lo, hi, "up_sb%d" % i))
+
+        for a in range(2):
+            for q in range(4):
+                nc.sync.dma_start(
+                    out=down_planes[32 * q : 32 * q + 16, a, :].bitcast(I32),
+                    in_=down_scales[4 * a : 4 * a + 4, 4 * q : 4 * q + 4, :].bitcast(I32),
+                )
+        down_sb = {}
+        for nh in range(N_HALVES):
+            for a in range(2):
+                d_t = keep.tile([P, 4, N_TILE], U32, name="down_sb%d_%d" % (nh, a), align_bytes=64)
+                nc.sync.dma_start(
+                    out=d_t[:].bitcast(I32),
+                    in_=down_view[
+                        :, 4 * a : 4 * a + 4, 4 * N_TILE * nh : 4 * N_TILE * (nh + 1)
+                    ].bitcast(I32),
+                )
+                down_sb[(nh, a)] = d_t
+
+        def weight_slice(tiles, c):
+            for i, (lo, hi) in enumerate(LOAD_COLS):
+                if lo <= c * K_PASS < hi:
+                    return tiles[i], c * K_PASS - lo
+            raise ValueError("no such chunk")
+
+        x_codes = []
+        x_scales = []
+        x_banks = []
+        for mt in range(M_TILES):
+            xt = psum.tile([P, D_GROUPS, 2, P], F32, tag="tr", bufs=2, name="xt")
+            words = x_sb[mt][:].bitcast(F32)
+            for g in range(D_GROUPS):
+                for u in range(2):
+                    nc.tensor.transpose(
+                        xt[:, g, u, :], words[:, 256 * g + u : 256 * (g + 1) : 2], ident_f[:]
+                    )
+            x_banks.append(xt)
+        for mt in range(M_TILES):
+            xg = keep.tile([P, D_GROUPS * P * 4], BF16, name="xg%d" % mt, align_bytes=64)
+            dst = xg[:].bitcast(F32).rearrange("p (g m u) -> p g m u", g=D_GROUPS, u=2)
+            src = x_banks[mt][:].rearrange("p g u m -> p g m u")
+            if mt == 0:
+                nc.vector.tensor_copy(out=dst, in_=src)
+            else:
+                nc.scalar.copy(out=dst, in_=src)
+            xq = keep.tile([P, D_GROUPS, P], U32, name="xq%d" % mt, align_bytes=64)
+            xs = keep.tile([P, D_GROUPS, P], U8, name="xs%d" % mt, align_bytes=64)
+            nc.vector.quantize_mx(
+                out=xq[:].rearrange("p g m -> p (g m)").bitcast(FP8X4),
+                scales=xs[:].rearrange("p g m -> p (g m)"),
+                in_=xg[:],
+            )
+            x_codes.append(xq)
+            x_scales.append(xs)
+
+        def project(acc, mt, tiles, planes, first, c):
+            w_t, at = weight_slice(tiles, c)
+            for g in range(D_GROUPS):
+                nc.tensor.matmul_mx(
+                    out=acc[:],
+                    lhsT=x_codes[mt][:, g, :].bitcast(FP8X4),
+                    lhsT_scale=x_scales[mt][:, g, :],
+                    rhs=w_t[:, g, at : at + K_PASS].bitcast(FP8X4),
+                    rhs_scale=planes[first + 4 * g : P, c * K_PASS : (c + 1) * K_PASS],
+                    start=(g == 0),
+                    stop=(g == D_GROUPS - 1),
+                )
+
+        hidden = {}
+
+        def stage1(c):
+            g_ps = []
+            u_ps = []
+            for mt in range(M_TILES):
+                acc = psum.tile([P, K_PASS], F32, tag="g", bufs=3, name="g_ps")
+                project(acc, mt, gate_sb, gate_planes, 0, c)
+                g_ps.append(acc)
+            for mt in range(M_TILES):
+                acc = psum.tile([P, K_PASS], F32, tag="u", bufs=3, name="u_ps")
+                project(acc, mt, up_sb, up_planes, 8, c)
+                u_ps.append(acc)
+            for mt in range(M_TILES):
+                sg = work.tile([P, 4, P], F32, tag="sg", bufs=3, name="sg")
+                nc.scalar.activation(
+                    out=sg[:], in_=g_ps[mt][:].rearrange("m (p t) -> m t p", t=4), func=silu
+                )
+                h_sb = work.tile([P, 4, P], BF16, tag="h", bufs=6, name="h_sb")
+                nc.vector.tensor_tensor(
+                    out=h_sb[:],
+                    in0=sg[:],
+                    in1=u_ps[mt][:].rearrange("m (p t) -> m t p", t=4),
+                    op=mult,
+                )
+                hidden[(c, mt)] = h_sb
+
+        h_codes = {}
+        h_scales = {}
+
+        def flip(c, tags):
+            banks = []
+            for mt in range(M_TILES):
+                tr = psum.tile(
+                    [P, 4, P], BF16, tag=tags[mt], bufs=(2 if tags[mt] == "tr" else 3), name="tr"
+                )
+                for t in range(4):
+                    nc.tensor.transpose(tr[:, t, :], hidden[(c, mt)][:, t, :], ident_b[:])
+                banks.append(tr)
+            return banks
+
+        def quantise(c, banks):
+            hg = work.tile([P, M_TILES, P, 4], BF16, tag="hg", bufs=3, name="hg", align_bytes=64)
+            nc.scalar.copy(out=hg[:, 0], in_=banks[0][:].rearrange("p t m -> p m t"))
+            nc.vector.tensor_copy(out=hg[:, 1], in_=banks[1][:].rearrange("p t m -> p m t"))
+            hq = keep.tile([P, M_TILES, P], U32, name="hq%d" % c, align_bytes=64)
+            hs = keep.tile([P, M_TILES, P], U8, name="hs%d" % c, align_bytes=64)
+            nc.vector.quantize_mx(
+                out=hq[:].rearrange("p a m -> p (a m)").bitcast(FP8X4),
+                scales=hs[:].rearrange("p a m -> p (a m)"),
+                in_=hg[:].rearrange("p a m t -> p (a m t)"),
+            )
+            h_codes[c] = hq
+            h_scales[c] = hs
+
+        for c in range(F_GROUPS - 1):
+            stage1(c)
+            if c >= 1:
+                quantise(c - 1, flip(c - 1, ("tr", "tr")))
+        last = F_GROUPS - 1
+        stage1(last)
+        banks_a = flip(last - 1, ("tr", "tr"))
+        banks_b = flip(last, ("g", "u"))
+        quantise(last - 1, banks_a)
+        quantise(last, banks_b)
+
+        def down_pass(acc, mt, nh, g):
+            nc.tensor.matmul_mx(
+                out=acc[:],
+                lhsT=h_codes[g][:, mt, :].bitcast(FP8X4),
+                lhsT_scale=h_scales[g][:, mt, :],
+                rhs=down_sb[(nh, g // 4)][:, g % 4, :].bitcast(FP8X4),
+                rhs_scale=down_planes[
+                    4 * (g % 4) : P, g // 4, nh * N_TILE : (nh + 1) * N_TILE
+                ],
+                start=(g == 0),
+                stop=(g == F_GROUPS - 1),
+            )
+
+        def store(acc, mt, nh, on_scalar):
+            o_sb = work.tile([P, N_TILE], F32, tag="o", bufs=4, name="o_sb")
+            if on_scalar:
+                nc.scalar.copy(out=o_sb[:], in_=acc[:])
+            else:
+                nc.vector.tensor_copy(out=o_sb[:], in_=acc[:])
+            nc.sync.dma_start(
+                out=out[mt * P : (mt + 1) * P, nh * N_TILE : (nh + 1) * N_TILE], in_=o_sb[:]
+            )
+
+        acc_a = psum.tile([P, N_TILE], F32, tag="g", bufs=3, name="acc_a")
+        acc_b = psum.tile([P, N_TILE], F32, tag="u", bufs=3, name="acc_b")
+        for g in range(F_GROUPS):
+            down_pass(acc_a, 0, 0, g)
+            down_pass(acc_b, 1, 0, g)
+        store(acc_a, 0, 0, True)
+        store(acc_b, 1, 0, False)
+        acc_c = psum.tile([P, N_TILE], F32, tag="g", bufs=3, name="acc_c")
+        for g in range(F_GROUPS):
+            down_pass(acc_c, 0, 1, g)
+        store(acc_c, 0, 1, True)
+        acc_d = psum.tile([P, N_TILE], F32, tag="u", bufs=3, name="acc_d")
+        for g in range(F_GROUPS):
+            down_pass(acc_d, 1, 1, g)
+        store(acc_d, 1, 1, False)

@@ -21,7 +21,8 @@ N_HALVES = D // N_TILE
 
 FLOPS = 2 * M * D * F * 3
 
-LOAD_COLS = ((0, 512), (512, 1024), (1024, 2048), (2048, 3072), (3072, 4096))
+EARLY = 2
+TAIL_GROUPS = 2
 
 
 def tile_mlp_kernel(
@@ -30,6 +31,7 @@ def tile_mlp_kernel(
     nc = tc.nc
     silu = mybir.ActivationFunctionType.Silu
     mult = mybir.AluOpType.mult
+    split = EARLY * K_PASS
 
     with ExitStack() as ctx:
         keep = ctx.enter_context(tc.tile_pool(name="keep", bufs=1))
@@ -37,22 +39,24 @@ def tile_mlp_kernel(
         psum = ctx.enter_context(tc.psum_pool(name="psum", bufs=1))
         ctx.enter_context(tc.manual_schedule())
 
+        ident_f = keep.tile([P, P], F32)
+        make_identity(nc, ident_f[:])
+        ident_b = keep.tile([P, P], BF16)
+        make_identity(nc, ident_b[:])
+
         warm_in = keep.tile([P, 8], F32)
         warm_out = keep.tile([P, 8], F32)
         nc.vector.memset(warm_in[:], 0.0)
         nc.scalar.activation(out=warm_out[:], in_=warm_in[:], func=silu)
 
-        gate_planes = keep.tile([P, F], U8, align_bytes=64)
-        up_planes = keep.tile([P, F], U8, align_bytes=64)
+        gate_pl_a = keep.tile([P, split], U8, align_bytes=64)
+        up_pl_a = keep.tile([P, split], U8, align_bytes=64)
+        gate_pl_b = keep.tile([P, F - split], U8, align_bytes=64)
+        up_pl_b = keep.tile([P, F - split], U8, align_bytes=64)
         down_planes = keep.tile([P, 2, D], U8, align_bytes=64)
-        nc.vector.memset(gate_planes[:].bitcast(I32), 0)
-        nc.vector.memset(up_planes[:].bitcast(I32), 0)
+        for pl in (gate_pl_a, up_pl_a, gate_pl_b, up_pl_b):
+            nc.vector.memset(pl[:].bitcast(I32), 0)
         nc.vector.memset(down_planes[:].rearrange("p a n -> p (a n)").bitcast(I32), 0)
-
-        ident_f = keep.tile([P, P], F32)
-        make_identity(nc, ident_f[:])
-        ident_b = keep.tile([P, P], BF16)
-        make_identity(nc, ident_b[:])
 
         x_sb = []
         for mt in range(M_TILES):
@@ -60,57 +64,58 @@ def tile_mlp_kernel(
             nc.sync.dma_start(out=x_t[:], in_=x[mt * P : (mt + 1) * P, :])
             x_sb.append(x_t)
 
-        def load_planes(planes, scales, first):
+        def load_planes_early(planes, scales, first):
             for q in range(4):
                 nc.sync.dma_start(
                     out=planes[32 * q + first : 32 * q + first + 8, :].bitcast(I32),
-                    in_=scales[:, 4 * q : 4 * q + 4, :].bitcast(I32),
+                    in_=scales[:, 4 * q : 4 * q + 4, 0:split].bitcast(I32),
+                )
+
+        def load_planes_late(planes, scales, first):
+            for q in range(4):
+                nc.gpsimd.dma_start(
+                    out=planes[32 * q + first : 32 * q + first + 8, :].bitcast(F32),
+                    in_=scales[:, 4 * q : 4 * q + 4, split:F].bitcast(F32),
+                )
+
+        load_planes_late(gate_pl_b, gate_scales, 0)
+        load_planes_late(up_pl_b, up_scales, 8)
+        for a in range(2):
+            for q in range(4):
+                nc.gpsimd.dma_start(
+                    out=down_planes[32 * q : 32 * q + 16, a, :].bitcast(F32),
+                    in_=down_scales[4 * a : 4 * a + 4, 4 * q : 4 * q + 4, :].bitcast(F32),
                 )
 
         gate_view = gate_words.rearrange("g p n t -> p g (n t)")
         up_view = up_words.rearrange("g p n t -> p g (n t)")
-        down_view = down_words.rearrange("g p n t -> p g (n t)")
 
-        def load_words(view, lo, hi, name):
-            w_t = keep.tile([P, D_GROUPS, hi - lo], U32, name=name, align_bytes=64)
+        def load_words(view, c, name):
+            w_t = keep.tile([P, D_GROUPS, K_PASS], U32, name=name, align_bytes=64)
             nc.sync.dma_start(
-                out=w_t[:].bitcast(I32), in_=view[:, :, 4 * lo : 4 * hi].bitcast(I32)
+                out=w_t[:].bitcast(I32),
+                in_=view[:, :, 4 * K_PASS * c : 4 * K_PASS * (c + 1)].bitcast(I32),
             )
             return w_t
 
         gate_sb = []
         up_sb = []
-        for i, (lo, hi) in enumerate(LOAD_COLS):
-            if i == 0:
-                load_planes(gate_planes, gate_scales, 0)
-            gate_sb.append(load_words(gate_view, lo, hi, "gate_sb%d" % i))
-            if i == 0:
-                load_planes(up_planes, up_scales, 8)
-            up_sb.append(load_words(up_view, lo, hi, "up_sb%d" % i))
+        for c in range(F_GROUPS):
+            if c == 0:
+                load_planes_early(gate_pl_a, gate_scales, 0)
+            gate_sb.append(load_words(gate_view, c, "gate_sb%d" % c))
+            if c == 0:
+                load_planes_early(up_pl_a, up_scales, 8)
+            up_sb.append(load_words(up_view, c, "up_sb%d" % c))
 
-        for a in range(2):
-            for q in range(4):
-                nc.sync.dma_start(
-                    out=down_planes[32 * q : 32 * q + 16, a, :].bitcast(I32),
-                    in_=down_scales[4 * a : 4 * a + 4, 4 * q : 4 * q + 4, :].bitcast(I32),
-                )
-        down_sb = {}
-        for nh in range(N_HALVES):
-            for a in range(2):
-                d_t = keep.tile([P, 4, N_TILE], U32, name="down_sb%d_%d" % (nh, a), align_bytes=64)
-                nc.sync.dma_start(
-                    out=d_t[:].bitcast(I32),
-                    in_=down_view[
-                        :, 4 * a : 4 * a + 4, 4 * N_TILE * nh : 4 * N_TILE * (nh + 1)
-                    ].bitcast(I32),
-                )
-                down_sb[(nh, a)] = d_t
-
-        def weight_slice(tiles, c):
-            for i, (lo, hi) in enumerate(LOAD_COLS):
-                if lo <= c * K_PASS < hi:
-                    return tiles[i], c * K_PASS - lo
-            raise ValueError("no such chunk")
+        down_sb = []
+        for g in range(F_GROUPS):
+            d_t = keep.tile([P, D], U32, name="down_sb%d" % g, align_bytes=64)
+            nc.sync.dma_start(
+                out=d_t[:].bitcast(I32),
+                in_=down_words[g].rearrange("p n t -> p (n t)").bitcast(I32),
+            )
+            down_sb.append(d_t)
 
         x_codes = []
         x_scales = []
@@ -142,91 +147,100 @@ def tile_mlp_kernel(
             x_codes.append(xq)
             x_scales.append(xs)
 
-        def project(acc, mt, tiles, planes, first, c):
-            w_t, at = weight_slice(tiles, c)
-            for g in range(D_GROUPS):
-                nc.tensor.matmul_mx(
-                    out=acc[:],
-                    lhsT=x_codes[mt][:, g, :].bitcast(FP8X4),
-                    lhsT_scale=x_scales[mt][:, g, :],
-                    rhs=w_t[:, g, at : at + K_PASS].bitcast(FP8X4),
-                    rhs_scale=planes[first + 4 * g : P, c * K_PASS : (c + 1) * K_PASS],
-                    start=(g == 0),
-                    stop=(g == D_GROUPS - 1),
+        def project(tag, words_sb, pl_a, pl_b, first, c):
+            planes, at = (pl_a, c * K_PASS) if c < EARLY else (pl_b, (c - EARLY) * K_PASS)
+            banks = []
+            for mt in range(M_TILES):
+                acc = psum.tile([P, K_PASS], F32, tag=tag, bufs=3, name="acc_" + tag)
+                for g in range(D_GROUPS):
+                    nc.tensor.matmul_mx(
+                        out=acc[:],
+                        lhsT=x_codes[mt][:, g, :].bitcast(FP8X4),
+                        lhsT_scale=x_scales[mt][:, g, :],
+                        rhs=words_sb[c][:, g, :].bitcast(FP8X4),
+                        rhs_scale=planes[first + 4 * g : P, at : at + K_PASS],
+                        start=(g == 0),
+                        stop=(g == D_GROUPS - 1),
+                    )
+                banks.append(acc)
+            return banks
+
+        def gate_part(c):
+            banks = project("g", gate_sb, gate_pl_a, gate_pl_b, 0, c)
+            acts = []
+            for mt in range(M_TILES):
+                sg = work.tile([P, 4, P], F32, tag="sg", bufs=4, name="sg")
+                nc.scalar.activation(
+                    out=sg[:], in_=banks[mt][:].rearrange("m (p t) -> m t p", t=4), func=silu
                 )
+                acts.append(sg)
+            return acts
 
         hidden = {}
 
-        def stage1(c):
-            g_ps = []
-            u_ps = []
+        def up_part(c, acts):
+            banks = project("u", up_sb, up_pl_a, up_pl_b, 8, c)
             for mt in range(M_TILES):
-                acc = psum.tile([P, K_PASS], F32, tag="g", bufs=3, name="g_ps")
-                project(acc, mt, gate_sb, gate_planes, 0, c)
-                g_ps.append(acc)
-            for mt in range(M_TILES):
-                acc = psum.tile([P, K_PASS], F32, tag="u", bufs=3, name="u_ps")
-                project(acc, mt, up_sb, up_planes, 8, c)
-                u_ps.append(acc)
-            for mt in range(M_TILES):
-                sg = work.tile([P, 4, P], F32, tag="sg", bufs=3, name="sg")
-                nc.scalar.activation(
-                    out=sg[:], in_=g_ps[mt][:].rearrange("m (p t) -> m t p", t=4), func=silu
-                )
-                h_sb = work.tile([P, 4, P], BF16, tag="h", bufs=6, name="h_sb")
+                h_sb = work.tile([P, 4, P], BF16, tag="h", bufs=8, name="h_sb")
                 nc.vector.tensor_tensor(
                     out=h_sb[:],
-                    in0=sg[:],
-                    in1=u_ps[mt][:].rearrange("m (p t) -> m t p", t=4),
+                    in0=acts[mt][:],
+                    in1=banks[mt][:].rearrange("m (p t) -> m t p", t=4),
                     op=mult,
                 )
                 hidden[(c, mt)] = h_sb
 
+        grouped = {}
+
+        def flip_pair(c0):
+            banks = []
+            for c in (c0, c0 + 1):
+                tr = psum.tile([P, M_TILES, 4, P], BF16, tag="tr", bufs=2, name="tr")
+                for mt in range(M_TILES):
+                    for t in range(4):
+                        nc.tensor.transpose(tr[:, mt, t, :], hidden[(c, mt)][:, t, :], ident_b[:])
+                banks.append(tr)
+            for i, c in enumerate((c0, c0 + 1)):
+                hg = work.tile([P, M_TILES, P, 4], BF16, tag="hg", bufs=4, name="hg", align_bytes=64)
+                src = banks[i][:].rearrange("p a t m -> p a m t")
+                if i == 0:
+                    nc.scalar.copy(out=hg[:], in_=src)
+                else:
+                    nc.vector.tensor_copy(out=hg[:], in_=src)
+                grouped[c] = hg
+
         h_codes = {}
         h_scales = {}
 
-        def flip(c, tags):
-            banks = []
-            for mt in range(M_TILES):
-                tr = psum.tile(
-                    [P, 4, P], BF16, tag=tags[mt], bufs=(2 if tags[mt] == "tr" else 3), name="tr"
-                )
-                for t in range(4):
-                    nc.tensor.transpose(tr[:, t, :], hidden[(c, mt)][:, t, :], ident_b[:])
-                banks.append(tr)
-            return banks
-
-        def quantise(c, banks):
-            hg = work.tile([P, M_TILES, P, 4], BF16, tag="hg", bufs=3, name="hg", align_bytes=64)
-            nc.scalar.copy(out=hg[:, 0], in_=banks[0][:].rearrange("p t m -> p m t"))
-            nc.vector.tensor_copy(out=hg[:, 1], in_=banks[1][:].rearrange("p t m -> p m t"))
+        def quantise(c):
             hq = keep.tile([P, M_TILES, P], U32, name="hq%d" % c, align_bytes=64)
             hs = keep.tile([P, M_TILES, P], U8, name="hs%d" % c, align_bytes=64)
             nc.vector.quantize_mx(
                 out=hq[:].rearrange("p a m -> p (a m)").bitcast(FP8X4),
                 scales=hs[:].rearrange("p a m -> p (a m)"),
-                in_=hg[:].rearrange("p a m t -> p (a m t)"),
+                in_=grouped[c][:].rearrange("p a m t -> p (a m t)"),
             )
             h_codes[c] = hq
             h_scales[c] = hs
 
-        for c in range(F_GROUPS - 1):
-            stage1(c)
-            if c >= 1:
-                quantise(c - 1, flip(c - 1, ("tr", "tr")))
-        last = F_GROUPS - 1
-        stage1(last)
-        banks_a = flip(last - 1, ("tr", "tr"))
-        banks_b = flip(last, ("g", "u"))
-        quantise(last - 1, banks_a)
-        quantise(last, banks_b)
+        for c in range(F_GROUPS):
+            acts = gate_part(c)
+            if c >= 2 and c % 2 == 0:
+                flip_pair(c - 2)
+            up_part(c, acts)
+            if c >= 2 and c % 2 == 0:
+                quantise(c - 2)
+                quantise(c - 1)
+        flip_pair(F_GROUPS - 2)
+        quantise(F_GROUPS - 2)
+        quantise(F_GROUPS - 1)
 
         def down_pass(acc, mt, nh, g):
             nc.tensor.matmul_mx(
                 out=acc[:],
                 lhsT=h_codes[g][:, mt, :].bitcast(FP8X4),
                 lhsT_scale=h_scales[g][:, mt, :],
-                rhs=down_sb[(nh, g // 4)][:, g % 4, :].bitcast(FP8X4),
+                rhs=down_sb[g][:, nh * N_TILE : (nh + 1) * N_TILE].bitcast(FP8X4),
                 rhs_scale=down_planes[
                     4 * (g % 4) : P, g // 4, nh * N_TILE : (nh + 1) * N_TILE
                 ],
@@ -234,28 +248,22 @@ def tile_mlp_kernel(
                 stop=(g == F_GROUPS - 1),
             )
 
-        def store(acc, mt, nh, on_scalar):
+        outs = []
+        for i, (mt, nh) in enumerate(((0, 0), (1, 0), (0, 1), (1, 1))):
+            tag = "g" if i % 2 == 0 else "u"
+            acc = psum.tile([P, N_TILE], F32, tag=tag, bufs=3, name="acc_o")
+            outs.append((acc, mt, nh))
+        for g in range(F_GROUPS - TAIL_GROUPS):
+            for acc, mt, nh in outs:
+                down_pass(acc, mt, nh, g)
+        for i, (acc, mt, nh) in enumerate(outs):
+            for g in range(F_GROUPS - TAIL_GROUPS, F_GROUPS):
+                down_pass(acc, mt, nh, g)
             o_sb = work.tile([P, N_TILE], F32, tag="o", bufs=4, name="o_sb")
-            if on_scalar:
+            if i % 2 == 0:
                 nc.scalar.copy(out=o_sb[:], in_=acc[:])
             else:
                 nc.vector.tensor_copy(out=o_sb[:], in_=acc[:])
             nc.sync.dma_start(
                 out=out[mt * P : (mt + 1) * P, nh * N_TILE : (nh + 1) * N_TILE], in_=o_sb[:]
             )
-
-        acc_a = psum.tile([P, N_TILE], F32, tag="g", bufs=3, name="acc_a")
-        acc_b = psum.tile([P, N_TILE], F32, tag="u", bufs=3, name="acc_b")
-        for g in range(F_GROUPS):
-            down_pass(acc_a, 0, 0, g)
-            down_pass(acc_b, 1, 0, g)
-        store(acc_a, 0, 0, True)
-        store(acc_b, 1, 0, False)
-        acc_c = psum.tile([P, N_TILE], F32, tag="g", bufs=3, name="acc_c")
-        for g in range(F_GROUPS):
-            down_pass(acc_c, 0, 1, g)
-        store(acc_c, 0, 1, True)
-        acc_d = psum.tile([P, N_TILE], F32, tag="u", bufs=3, name="acc_d")
-        for g in range(F_GROUPS):
-            down_pass(acc_d, 1, 1, g)
-        store(acc_d, 1, 1, False)

@@ -17,11 +17,11 @@ K_PASS = 512
 D_GROUPS = D // K_PASS
 F_GROUPS = F // K_PASS
 N_TILE = 512
-N_HALVES = D // N_TILE
 
 FLOPS = 2 * M * D * F * 3
 
-EARLY = 2
+GATE_BATCHES = ((0, 2, "sync"), (2, 4, "sync"), (4, 6, "sync"), (6, 8, "gpsimd"))
+UP_BATCHES = ((0, 2, "sync"), (2, 8, "gpsimd"))
 TAIL_GROUPS = 2
 
 
@@ -31,7 +31,6 @@ def tile_mlp_kernel(
     nc = tc.nc
     silu = mybir.ActivationFunctionType.Silu
     mult = mybir.AluOpType.mult
-    split = EARLY * K_PASS
 
     with ExitStack() as ctx:
         keep = ctx.enter_context(tc.tile_pool(name="keep", bufs=1))
@@ -49,43 +48,46 @@ def tile_mlp_kernel(
         nc.vector.memset(warm_in[:], 0.0)
         nc.scalar.activation(out=warm_out[:], in_=warm_in[:], func=silu)
 
-        gate_pl_a = keep.tile([P, split], U8, align_bytes=64)
-        up_pl_a = keep.tile([P, split], U8, align_bytes=64)
-        gate_pl_b = keep.tile([P, F - split], U8, align_bytes=64)
-        up_pl_b = keep.tile([P, F - split], U8, align_bytes=64)
-        down_planes = keep.tile([P, 2, D], U8, align_bytes=64)
-        for pl in (gate_pl_a, up_pl_a, gate_pl_b, up_pl_b):
+        def plane_tiles(batches, name):
+            return [
+                keep.tile([P, (hi - lo) * K_PASS], U8, name="%s%d" % (name, lo), align_bytes=64)
+                for lo, hi, queue in batches
+            ]
+
+        gate_pl = plane_tiles(GATE_BATCHES, "gate_pl")
+        up_pl = plane_tiles(UP_BATCHES, "up_pl")
+        down_pl = [keep.tile([P, D], U8, name="down_pl%d" % a, align_bytes=64) for a in range(2)]
+        for pl in (up_pl[1], gate_pl[0], up_pl[0], gate_pl[3], gate_pl[1], gate_pl[2], down_pl[1], down_pl[0]):
             nc.vector.memset(pl[:].bitcast(I32), 0)
-        nc.vector.memset(down_planes[:].rearrange("p a n -> p (a n)").bitcast(I32), 0)
+
+        def load_planes(planes, scales, batch):
+            lo, hi, queue = batch
+            for q in range(4):
+                dst = planes[32 * q : 32 * q + 8, :]
+                src = scales[:, 4 * q : 4 * q + 4, lo * K_PASS : hi * K_PASS]
+                if queue == "sync":
+                    nc.sync.dma_start(out=dst.bitcast(I32), in_=src.bitcast(I32))
+                else:
+                    nc.gpsimd.dma_start(out=dst.bitcast(F32), in_=src.bitcast(F32))
+
+        def load_down_planes(a, queue):
+            for q in range(4):
+                dst = down_pl[a][32 * q : 32 * q + 16, :]
+                src = down_scales[4 * a : 4 * a + 4, 4 * q : 4 * q + 4, :]
+                if queue == "sync":
+                    nc.sync.dma_start(out=dst.bitcast(I32), in_=src.bitcast(I32))
+                else:
+                    nc.gpsimd.dma_start(out=dst.bitcast(F32), in_=src.bitcast(F32))
+
+        load_planes(up_pl[1], up_scales, UP_BATCHES[1])
+        load_planes(gate_pl[3], gate_scales, GATE_BATCHES[3])
+        load_down_planes(1, "gpsimd")
 
         x_sb = []
         for mt in range(M_TILES):
             x_t = keep.tile([P, D], BF16, name="x_sb%d" % mt)
             nc.sync.dma_start(out=x_t[:], in_=x[mt * P : (mt + 1) * P, :])
             x_sb.append(x_t)
-
-        def load_planes_early(planes, scales, first):
-            for q in range(4):
-                nc.sync.dma_start(
-                    out=planes[32 * q + first : 32 * q + first + 8, :].bitcast(I32),
-                    in_=scales[:, 4 * q : 4 * q + 4, 0:split].bitcast(I32),
-                )
-
-        def load_planes_late(planes, scales, first):
-            for q in range(4):
-                nc.gpsimd.dma_start(
-                    out=planes[32 * q + first : 32 * q + first + 8, :].bitcast(F32),
-                    in_=scales[:, 4 * q : 4 * q + 4, split:F].bitcast(F32),
-                )
-
-        load_planes_late(gate_pl_b, gate_scales, 0)
-        load_planes_late(up_pl_b, up_scales, 8)
-        for a in range(2):
-            for q in range(4):
-                nc.gpsimd.dma_start(
-                    out=down_planes[32 * q : 32 * q + 16, a, :].bitcast(F32),
-                    in_=down_scales[4 * a : 4 * a + 4, 4 * q : 4 * q + 4, :].bitcast(F32),
-                )
 
         gate_view = gate_words.rearrange("g p n t -> p g (n t)")
         up_view = up_words.rearrange("g p n t -> p g (n t)")
@@ -101,13 +103,16 @@ def tile_mlp_kernel(
         gate_sb = []
         up_sb = []
         for c in range(F_GROUPS):
-            if c == 0:
-                load_planes_early(gate_pl_a, gate_scales, 0)
+            for i, batch in enumerate(GATE_BATCHES):
+                if batch[0] == c and batch[2] == "sync":
+                    load_planes(gate_pl[i], gate_scales, batch)
             gate_sb.append(load_words(gate_view, c, "gate_sb%d" % c))
-            if c == 0:
-                load_planes_early(up_pl_a, up_scales, 8)
+            for i, batch in enumerate(UP_BATCHES):
+                if batch[0] == c and batch[2] == "sync":
+                    load_planes(up_pl[i], up_scales, batch)
             up_sb.append(load_words(up_view, c, "up_sb%d" % c))
 
+        load_down_planes(0, "sync")
         down_sb = []
         for g in range(F_GROUPS):
             d_t = keep.tile([P, D], U32, name="down_sb%d" % g, align_bytes=64)
@@ -147,8 +152,11 @@ def tile_mlp_kernel(
             x_codes.append(xq)
             x_scales.append(xs)
 
-        def project(tag, words_sb, pl_a, pl_b, first, c):
-            planes, at = (pl_a, c * K_PASS) if c < EARLY else (pl_b, (c - EARLY) * K_PASS)
+        def project(tag, words_sb, batches, tiles, c):
+            planes, at = None, 0
+            for i, (lo, hi, queue) in enumerate(batches):
+                if lo <= c < hi:
+                    planes, at = tiles[i], (c - lo) * K_PASS
             banks = []
             for mt in range(M_TILES):
                 acc = psum.tile([P, K_PASS], F32, tag=tag, bufs=3, name="acc_" + tag)
@@ -158,7 +166,7 @@ def tile_mlp_kernel(
                         lhsT=x_codes[mt][:, g, :].bitcast(FP8X4),
                         lhsT_scale=x_scales[mt][:, g, :],
                         rhs=words_sb[c][:, g, :].bitcast(FP8X4),
-                        rhs_scale=planes[first + 4 * g : P, at : at + K_PASS],
+                        rhs_scale=planes[4 * g : P, at : at + K_PASS],
                         start=(g == 0),
                         stop=(g == D_GROUPS - 1),
                     )
@@ -166,7 +174,7 @@ def tile_mlp_kernel(
             return banks
 
         def gate_part(c):
-            banks = project("g", gate_sb, gate_pl_a, gate_pl_b, 0, c)
+            banks = project("g", gate_sb, GATE_BATCHES, gate_pl, c)
             acts = []
             for mt in range(M_TILES):
                 sg = work.tile([P, 4, P], F32, tag="sg", bufs=4, name="sg")
@@ -179,7 +187,7 @@ def tile_mlp_kernel(
         hidden = {}
 
         def up_part(c, acts):
-            banks = project("u", up_sb, up_pl_a, up_pl_b, 8, c)
+            banks = project("u", up_sb, UP_BATCHES, up_pl, c)
             for mt in range(M_TILES):
                 h_sb = work.tile([P, 4, P], BF16, tag="h", bufs=8, name="h_sb")
                 nc.vector.tensor_tensor(
@@ -192,15 +200,15 @@ def tile_mlp_kernel(
 
         grouped = {}
 
-        def flip_pair(c0):
+        def flip(chunks):
             banks = []
-            for c in (c0, c0 + 1):
+            for c in chunks:
                 tr = psum.tile([P, M_TILES, 4, P], BF16, tag="tr", bufs=2, name="tr")
                 for mt in range(M_TILES):
                     for t in range(4):
                         nc.tensor.transpose(tr[:, mt, t, :], hidden[(c, mt)][:, t, :], ident_b[:])
                 banks.append(tr)
-            for i, c in enumerate((c0, c0 + 1)):
+            for i, c in enumerate(chunks):
                 hg = work.tile([P, M_TILES, P, 4], BF16, tag="hg", bufs=4, name="hg", align_bytes=64)
                 src = banks[i][:].rearrange("p a t m -> p a m t")
                 if i == 0:
@@ -212,28 +220,26 @@ def tile_mlp_kernel(
         h_codes = {}
         h_scales = {}
 
-        def quantise(c):
-            hq = keep.tile([P, M_TILES, P], U32, name="hq%d" % c, align_bytes=64)
-            hs = keep.tile([P, M_TILES, P], U8, name="hs%d" % c, align_bytes=64)
-            nc.vector.quantize_mx(
-                out=hq[:].rearrange("p a m -> p (a m)").bitcast(FP8X4),
-                scales=hs[:].rearrange("p a m -> p (a m)"),
-                in_=grouped[c][:].rearrange("p a m t -> p (a m t)"),
-            )
-            h_codes[c] = hq
-            h_scales[c] = hs
+        def quantise(chunks):
+            for c in chunks:
+                hq = keep.tile([P, M_TILES, P], U32, name="hq%d" % c, align_bytes=64)
+                hs = keep.tile([P, M_TILES, P], U8, name="hs%d" % c, align_bytes=64)
+                nc.vector.quantize_mx(
+                    out=hq[:].rearrange("p a m -> p (a m)").bitcast(FP8X4),
+                    scales=hs[:].rearrange("p a m -> p (a m)"),
+                    in_=grouped[c][:].rearrange("p a m t -> p (a m t)"),
+                )
+                h_codes[c] = hq
+                h_scales[c] = hs
 
+        flips = {1: (0,), 3: (1, 2), 5: (3, 4), 7: (5, 6)}
         for c in range(F_GROUPS):
             acts = gate_part(c)
-            if c >= 2 and c % 2 == 0:
-                flip_pair(c - 2)
+            if c in flips:
+                flip(flips[c])
             up_part(c, acts)
-            if c >= 2 and c % 2 == 0:
-                quantise(c - 2)
-                quantise(c - 1)
-        flip_pair(F_GROUPS - 2)
-        quantise(F_GROUPS - 2)
-        quantise(F_GROUPS - 1)
+            if c in flips:
+                quantise(flips[c])
 
         def down_pass(acc, mt, nh, g):
             nc.tensor.matmul_mx(
@@ -241,9 +247,7 @@ def tile_mlp_kernel(
                 lhsT=h_codes[g][:, mt, :].bitcast(FP8X4),
                 lhsT_scale=h_scales[g][:, mt, :],
                 rhs=down_sb[g][:, nh * N_TILE : (nh + 1) * N_TILE].bitcast(FP8X4),
-                rhs_scale=down_planes[
-                    4 * (g % 4) : P, g // 4, nh * N_TILE : (nh + 1) * N_TILE
-                ],
+                rhs_scale=down_pl[g // 4][4 * (g % 4) : P, nh * N_TILE : (nh + 1) * N_TILE],
                 start=(g == 0),
                 stop=(g == F_GROUPS - 1),
             )
@@ -256,6 +260,9 @@ def tile_mlp_kernel(
         for g in range(F_GROUPS - TAIL_GROUPS):
             for acc, mt, nh in outs:
                 down_pass(acc, mt, nh, g)
+            if g == 0:
+                flip((F_GROUPS - 1,))
+                quantise((F_GROUPS - 1,))
         for i, (acc, mt, nh) in enumerate(outs):
             for g in range(F_GROUPS - TAIL_GROUPS, F_GROUPS):
                 down_pass(acc, mt, nh, g)

@@ -20,7 +20,7 @@ N_TILE = 512
 
 FLOPS = 2 * M * D * F * 3
 
-GATE_BATCHES = ((0, 2, "sync"), (2, 4, "sync"), (4, 6, "sync"), (6, 8, "gpsimd"))
+GATE_BATCHES = ((0, 2, "sync"), (2, 5, "sync"), (5, 8, "gpsimd"))
 UP_BATCHES = ((0, 2, "sync"), (2, 8, "gpsimd"))
 TAIL_GROUPS = 2
 
@@ -57,7 +57,7 @@ def tile_mlp_kernel(
         gate_pl = plane_tiles(GATE_BATCHES, "gate_pl")
         up_pl = plane_tiles(UP_BATCHES, "up_pl")
         down_pl = [keep.tile([P, D], U8, name="down_pl%d" % a, align_bytes=64) for a in range(2)]
-        for pl in (up_pl[1], gate_pl[0], up_pl[0], gate_pl[3], gate_pl[1], gate_pl[2], down_pl[1], down_pl[0]):
+        for pl in (up_pl[1], gate_pl[0], up_pl[0], gate_pl[2], gate_pl[1], down_pl[0], down_pl[1]):
             nc.vector.memset(pl[:].bitcast(I32), 0)
 
         def load_planes(planes, scales, batch):
@@ -80,7 +80,8 @@ def tile_mlp_kernel(
                     nc.gpsimd.dma_start(out=dst.bitcast(F32), in_=src.bitcast(F32))
 
         load_planes(up_pl[1], up_scales, UP_BATCHES[1])
-        load_planes(gate_pl[3], gate_scales, GATE_BATCHES[3])
+        load_planes(gate_pl[2], gate_scales, GATE_BATCHES[2])
+        load_down_planes(0, "gpsimd")
         load_down_planes(1, "gpsimd")
 
         x_sb = []
@@ -112,15 +113,25 @@ def tile_mlp_kernel(
                     load_planes(up_pl[i], up_scales, batch)
             up_sb.append(load_words(up_view, c, "up_sb%d" % c))
 
-        load_down_planes(0, "sync")
-        down_sb = []
-        for g in range(F_GROUPS):
+        down_sb = {}
+        for g in range(F_GROUPS - TAIL_GROUPS):
             d_t = keep.tile([P, D], U32, name="down_sb%d" % g, align_bytes=64)
             nc.sync.dma_start(
                 out=d_t[:].bitcast(I32),
                 in_=down_words[g].rearrange("p n t -> p (n t)").bitcast(I32),
             )
-            down_sb.append(d_t)
+            for nh in range(2):
+                down_sb[(g, nh)] = (d_t, nh * N_TILE)
+        for nh in range(2):
+            for g in range(F_GROUPS - TAIL_GROUPS, F_GROUPS):
+                d_t = keep.tile([P, N_TILE], U32, name="down_sb%d_%d" % (g, nh), align_bytes=64)
+                nc.sync.dma_start(
+                    out=d_t[:].bitcast(I32),
+                    in_=down_words[g].rearrange("p n t -> p (n t)")[
+                        :, 4 * N_TILE * nh : 4 * N_TILE * (nh + 1)
+                    ].bitcast(I32),
+                )
+                down_sb[(g, nh)] = (d_t, 0)
 
         x_codes = []
         x_scales = []
@@ -241,36 +252,53 @@ def tile_mlp_kernel(
             if c in flips:
                 quantise(flips[c])
 
-        def down_pass(acc, mt, nh, g):
+        def down_pass(bank, g):
+            acc, mt, lo, width = bank
+            d_t, at = down_sb[(g, lo // N_TILE)]
+            at = at + lo % N_TILE
             nc.tensor.matmul_mx(
                 out=acc[:],
                 lhsT=h_codes[g][:, mt, :].bitcast(FP8X4),
                 lhsT_scale=h_scales[g][:, mt, :],
-                rhs=down_sb[g][:, nh * N_TILE : (nh + 1) * N_TILE].bitcast(FP8X4),
-                rhs_scale=down_pl[g // 4][4 * (g % 4) : P, nh * N_TILE : (nh + 1) * N_TILE],
+                rhs=d_t[:, at : at + width].bitcast(FP8X4),
+                rhs_scale=down_pl[g // 4][4 * (g % 4) : P, lo : lo + width],
                 start=(g == 0),
                 stop=(g == F_GROUPS - 1),
             )
 
-        outs = []
-        for i, (mt, nh) in enumerate(((0, 0), (1, 0), (0, 1), (1, 1))):
-            tag = "g" if i % 2 == 0 else "u"
-            acc = psum.tile([P, N_TILE], F32, tag=tag, bufs=3, name="acc_o")
-            outs.append((acc, mt, nh))
-        for g in range(F_GROUPS - TAIL_GROUPS):
-            for acc, mt, nh in outs:
-                down_pass(acc, mt, nh, g)
-            if g == 0:
-                flip((F_GROUPS - 1,))
-                quantise((F_GROUPS - 1,))
-        for i, (acc, mt, nh) in enumerate(outs):
-            for g in range(F_GROUPS - TAIL_GROUPS, F_GROUPS):
-                down_pass(acc, mt, nh, g)
-            o_sb = work.tile([P, N_TILE], F32, tag="o", bufs=4, name="o_sb")
-            if i % 2 == 0:
+        def store(bank, on_scalar):
+            acc, mt, lo, width = bank
+            o_sb = work.tile([P, width], F32, tag="o", bufs=5, name="o_sb")
+            if on_scalar:
                 nc.scalar.copy(out=o_sb[:], in_=acc[:])
             else:
                 nc.vector.tensor_copy(out=o_sb[:], in_=acc[:])
-            nc.sync.dma_start(
-                out=out[mt * P : (mt + 1) * P, nh * N_TILE : (nh + 1) * N_TILE], in_=o_sb[:]
-            )
+            nc.sync.dma_start(out=out[mt * P : (mt + 1) * P, lo : lo + width], in_=o_sb[:])
+
+        banks = []
+        for mt, lo, width, tag in (
+            (0, 0, 512, "g"),
+            (1, 0, 512, "u"),
+            (0, 512, 512, "g"),
+            (1, 512, 256, "u"),
+            (1, 768, 256, "g"),
+        ):
+            acc = psum.tile([P, width], F32, tag=tag, bufs=3, name="acc_o")
+            banks.append((acc, mt, lo, width))
+        for g in range(F_GROUPS - TAIL_GROUPS):
+            for bank in banks:
+                down_pass(bank, g)
+            if g == 0:
+                flip((F_GROUPS - 1,))
+                quantise((F_GROUPS - 1,))
+        tail = range(F_GROUPS - TAIL_GROUPS, F_GROUPS)
+        for i in range(2):
+            for g in tail:
+                down_pass(banks[i], g)
+            store(banks[i], i == 0)
+        for g in tail:
+            for bank in banks[2:]:
+                down_pass(bank, g)
+        store(banks[2], True)
+        store(banks[3], False)
+        store(banks[4], False)

@@ -17,11 +17,13 @@ K_PASS = 512
 D_GROUPS = D // K_PASS
 F_GROUPS = F // K_PASS
 N_TILE = 512
+PAIR = 2 * K_PASS
+N_PAIRS = F // PAIR
 
 FLOPS = 2 * M * D * F * 3
 
-GATE_BATCHES = ((0, 2, "sync"), (2, 5, "sync"), (5, 8, "gpsimd"))
-UP_BATCHES = ((0, 2, "sync"), (2, 8, "gpsimd"))
+GATE_BATCHES = ((0, 1, "sync"), (1, 2, "sync"), (2, 3, "sync"), (3, 4, "gpsimd"))
+UP_BATCHES = ((0, 1, "sync"), (1, 4, "gpsimd"))
 TAIL_GROUPS = 2
 
 
@@ -38,6 +40,9 @@ def tile_mlp_kernel(
         psum = ctx.enter_context(tc.psum_pool(name="psum", bufs=1))
         ctx.enter_context(tc.manual_schedule())
 
+        def bank(shape, dtype, name):
+            return psum.tile(shape, dtype, tag="bank", bufs=8, name=name)
+
         ident_f = keep.tile([P, P], F32)
         make_identity(nc, ident_f[:])
         ident_b = keep.tile([P, P], BF16)
@@ -50,21 +55,21 @@ def tile_mlp_kernel(
 
         def plane_tiles(batches, name):
             return [
-                keep.tile([P, (hi - lo) * K_PASS], U8, name="%s%d" % (name, lo), align_bytes=64)
+                keep.tile([P, (hi - lo) * PAIR], U8, name="%s%d" % (name, lo), align_bytes=64)
                 for lo, hi, queue in batches
             ]
 
         gate_pl = plane_tiles(GATE_BATCHES, "gate_pl")
         up_pl = plane_tiles(UP_BATCHES, "up_pl")
         down_pl = [keep.tile([P, D], U8, name="down_pl%d" % a, align_bytes=64) for a in range(2)]
-        for pl in (up_pl[1], gate_pl[0], up_pl[0], gate_pl[2], gate_pl[1], down_pl[0], down_pl[1]):
+        for pl in (up_pl[1], gate_pl[0], up_pl[0], gate_pl[3], gate_pl[1], gate_pl[2], down_pl[1], down_pl[0]):
             nc.vector.memset(pl[:].bitcast(I32), 0)
 
         def load_planes(planes, scales, batch):
             lo, hi, queue = batch
             for q in range(4):
                 dst = planes[32 * q : 32 * q + 8, :]
-                src = scales[:, 4 * q : 4 * q + 4, lo * K_PASS : hi * K_PASS]
+                src = scales[:, 4 * q : 4 * q + 4, lo * PAIR : hi * PAIR]
                 if queue == "sync":
                     nc.sync.dma_start(out=dst.bitcast(I32), in_=src.bitcast(I32))
                 else:
@@ -80,8 +85,7 @@ def tile_mlp_kernel(
                     nc.gpsimd.dma_start(out=dst.bitcast(F32), in_=src.bitcast(F32))
 
         load_planes(up_pl[1], up_scales, UP_BATCHES[1])
-        load_planes(gate_pl[2], gate_scales, GATE_BATCHES[2])
-        load_down_planes(0, "gpsimd")
+        load_planes(gate_pl[3], gate_scales, GATE_BATCHES[3])
         load_down_planes(1, "gpsimd")
 
         x_sb = []
@@ -90,29 +94,32 @@ def tile_mlp_kernel(
             nc.sync.dma_start(out=x_t[:], in_=x[mt * P : (mt + 1) * P, :])
             x_sb.append(x_t)
 
-        gate_view = gate_words.rearrange("g p n t -> p g (n t)")
-        up_view = up_words.rearrange("g p n t -> p g (n t)")
-
-        def load_words(view, c, name):
-            w_t = keep.tile([P, D_GROUPS, K_PASS], U32, name=name, align_bytes=64)
-            nc.sync.dma_start(
-                out=w_t[:].bitcast(I32),
-                in_=view[:, :, 4 * K_PASS * c : 4 * K_PASS * (c + 1)].bitcast(I32),
-            )
-            return w_t
+        def load_words(words, j, name):
+            tiles = []
+            for g in range(D_GROUPS):
+                w_t = keep.tile([P, PAIR], U32, name="%s%d_%d" % (name, j, g), align_bytes=64)
+                nc.sync.dma_start(
+                    out=w_t[:].bitcast(I32),
+                    in_=words[g].rearrange("p n t -> p (n t)")[
+                        :, 4 * PAIR * j : 4 * PAIR * (j + 1)
+                    ].bitcast(I32),
+                )
+                tiles.append(w_t)
+            return tiles
 
         gate_sb = []
         up_sb = []
-        for c in range(F_GROUPS):
+        for j in range(N_PAIRS):
             for i, batch in enumerate(GATE_BATCHES):
-                if batch[0] == c and batch[2] == "sync":
+                if batch[0] == j and batch[2] == "sync":
                     load_planes(gate_pl[i], gate_scales, batch)
-            gate_sb.append(load_words(gate_view, c, "gate_sb%d" % c))
+            gate_sb.append(load_words(gate_words, j, "gate_sb"))
             for i, batch in enumerate(UP_BATCHES):
-                if batch[0] == c and batch[2] == "sync":
+                if batch[0] == j and batch[2] == "sync":
                     load_planes(up_pl[i], up_scales, batch)
-            up_sb.append(load_words(up_view, c, "up_sb%d" % c))
+            up_sb.append(load_words(up_words, j, "up_sb"))
 
+        load_down_planes(0, "sync")
         down_sb = {}
         for g in range(F_GROUPS - TAIL_GROUPS):
             d_t = keep.tile([P, D], U32, name="down_sb%d" % g, align_bytes=64)
@@ -137,7 +144,7 @@ def tile_mlp_kernel(
         x_scales = []
         x_banks = []
         for mt in range(M_TILES):
-            xt = psum.tile([P, D_GROUPS, 2, P], F32, tag="tr", bufs=2, name="xt")
+            xt = bank([P, D_GROUPS, 2, P], F32, "xt")
             words = x_sb[mt][:].bitcast(F32)
             for g in range(D_GROUPS):
                 for u in range(2):
@@ -163,63 +170,67 @@ def tile_mlp_kernel(
             x_codes.append(xq)
             x_scales.append(xs)
 
-        def project(tag, words_sb, batches, tiles, c):
+        def units(j):
+            return [(2 * j + i, mt) for mt in range(M_TILES) for i in range(2)]
+
+        def project(words_sb, batches, tiles, j):
             planes, at = None, 0
             for i, (lo, hi, queue) in enumerate(batches):
-                if lo <= c < hi:
-                    planes, at = tiles[i], (c - lo) * K_PASS
-            banks = []
-            for mt in range(M_TILES):
-                acc = psum.tile([P, K_PASS], F32, tag=tag, bufs=3, name="acc_" + tag)
-                for g in range(D_GROUPS):
+                if lo <= j < hi:
+                    planes, at = tiles[i], (j - lo) * PAIR
+            accs = {}
+            for unit in units(j):
+                accs[unit] = bank([P, K_PASS], F32, "acc")
+            for g in range(D_GROUPS):
+                for c, mt in units(j):
+                    col = (c % 2) * K_PASS
                     nc.tensor.matmul_mx(
-                        out=acc[:],
+                        out=accs[(c, mt)][:],
                         lhsT=x_codes[mt][:, g, :].bitcast(FP8X4),
                         lhsT_scale=x_scales[mt][:, g, :],
-                        rhs=words_sb[c][:, g, :].bitcast(FP8X4),
-                        rhs_scale=planes[4 * g : P, at : at + K_PASS],
+                        rhs=words_sb[j][g][:, col : col + K_PASS].bitcast(FP8X4),
+                        rhs_scale=planes[4 * g : P, at + col : at + col + K_PASS],
                         start=(g == 0),
                         stop=(g == D_GROUPS - 1),
                     )
-                banks.append(acc)
-            return banks
+            return accs
 
-        def gate_part(c):
-            banks = project("g", gate_sb, GATE_BATCHES, gate_pl, c)
-            acts = []
-            for mt in range(M_TILES):
-                sg = work.tile([P, 4, P], F32, tag="sg", bufs=4, name="sg")
+        def gate_part(j):
+            accs = project(gate_sb, GATE_BATCHES, gate_pl, j)
+            acts = {}
+            for unit in units(j):
+                sg = work.tile([P, 4, P], F32, tag="sg", bufs=8, name="sg")
                 nc.scalar.activation(
-                    out=sg[:], in_=banks[mt][:].rearrange("m (p t) -> m t p", t=4), func=silu
+                    out=sg[:], in_=accs[unit][:].rearrange("m (p t) -> m t p", t=4), func=silu
                 )
-                acts.append(sg)
+                acts[unit] = sg
             return acts
 
         hidden = {}
 
-        def up_part(c, acts):
-            banks = project("u", up_sb, UP_BATCHES, up_pl, c)
-            for mt in range(M_TILES):
-                h_sb = work.tile([P, 4, P], BF16, tag="h", bufs=8, name="h_sb")
+        def up_part(j, acts):
+            accs = project(up_sb, UP_BATCHES, up_pl, j)
+            for unit in units(j):
+                h_sb = work.tile([P, 4, P], BF16, tag="h", bufs=12, name="h_sb")
                 nc.vector.tensor_tensor(
                     out=h_sb[:],
-                    in0=acts[mt][:],
-                    in1=banks[mt][:].rearrange("m (p t) -> m t p", t=4),
+                    in0=acts[unit][:],
+                    in1=accs[unit][:].rearrange("m (p t) -> m t p", t=4),
                     op=mult,
                 )
-                hidden[(c, mt)] = h_sb
+                hidden[unit] = h_sb
 
         grouped = {}
 
-        def flip(chunks):
+        def flip(j):
             banks = []
-            for c in chunks:
-                tr = psum.tile([P, M_TILES, 4, P], BF16, tag="tr", bufs=2, name="tr")
+            for c in (2 * j, 2 * j + 1):
+                tr = bank([P, M_TILES, 4, P], BF16, "tr")
                 for mt in range(M_TILES):
                     for t in range(4):
                         nc.tensor.transpose(tr[:, mt, t, :], hidden[(c, mt)][:, t, :], ident_b[:])
                 banks.append(tr)
-            for i, c in enumerate(chunks):
+            for i, c in enumerate((2 * j, 2 * j + 1)):
                 hg = work.tile([P, M_TILES, P, 4], BF16, tag="hg", bufs=4, name="hg", align_bytes=64)
                 src = banks[i][:].rearrange("p a t m -> p a m t")
                 if i == 0:
@@ -231,8 +242,8 @@ def tile_mlp_kernel(
         h_codes = {}
         h_scales = {}
 
-        def quantise(chunks):
-            for c in chunks:
+        def quantise(j):
+            for c in (2 * j, 2 * j + 1):
                 hq = keep.tile([P, M_TILES, P], U32, name="hq%d" % c, align_bytes=64)
                 hs = keep.tile([P, M_TILES, P], U8, name="hs%d" % c, align_bytes=64)
                 nc.vector.quantize_mx(
@@ -243,62 +254,52 @@ def tile_mlp_kernel(
                 h_codes[c] = hq
                 h_scales[c] = hs
 
-        flips = {1: (0,), 3: (1, 2), 5: (3, 4), 7: (5, 6)}
-        for c in range(F_GROUPS):
-            acts = gate_part(c)
-            if c in flips:
-                flip(flips[c])
-            up_part(c, acts)
-            if c in flips:
-                quantise(flips[c])
+        for j in range(N_PAIRS):
+            acts = gate_part(j)
+            if j >= 1:
+                flip(j - 1)
+            up_part(j, acts)
+            if j >= 1:
+                quantise(j - 1)
 
-        def down_pass(bank, g):
-            acc, mt, lo, width = bank
-            d_t, at = down_sb[(g, lo // N_TILE)]
-            at = at + lo % N_TILE
+        def down_pass(out_bank, g):
+            acc, mt, nh = out_bank
+            d_t, at = down_sb[(g, nh)]
             nc.tensor.matmul_mx(
                 out=acc[:],
                 lhsT=h_codes[g][:, mt, :].bitcast(FP8X4),
                 lhsT_scale=h_scales[g][:, mt, :],
-                rhs=d_t[:, at : at + width].bitcast(FP8X4),
-                rhs_scale=down_pl[g // 4][4 * (g % 4) : P, lo : lo + width],
+                rhs=d_t[:, at : at + N_TILE].bitcast(FP8X4),
+                rhs_scale=down_pl[g // 4][4 * (g % 4) : P, nh * N_TILE : (nh + 1) * N_TILE],
                 start=(g == 0),
                 stop=(g == F_GROUPS - 1),
             )
 
-        def store(bank, on_scalar):
-            acc, mt, lo, width = bank
-            o_sb = work.tile([P, width], F32, tag="o", bufs=5, name="o_sb")
+        def store(out_bank, on_scalar):
+            acc, mt, nh = out_bank
+            o_sb = work.tile([P, N_TILE], F32, tag="o", bufs=4, name="o_sb")
             if on_scalar:
                 nc.scalar.copy(out=o_sb[:], in_=acc[:])
             else:
                 nc.vector.tensor_copy(out=o_sb[:], in_=acc[:])
-            nc.sync.dma_start(out=out[mt * P : (mt + 1) * P, lo : lo + width], in_=o_sb[:])
+            nc.sync.dma_start(
+                out=out[mt * P : (mt + 1) * P, nh * N_TILE : (nh + 1) * N_TILE], in_=o_sb[:]
+            )
 
-        banks = []
-        for mt, lo, width, tag in (
-            (0, 0, 512, "g"),
-            (1, 0, 512, "u"),
-            (0, 512, 512, "g"),
-            (1, 512, 256, "u"),
-            (1, 768, 256, "g"),
-        ):
-            acc = psum.tile([P, width], F32, tag=tag, bufs=3, name="acc_o")
-            banks.append((acc, mt, lo, width))
+        outs = [(bank([P, N_TILE], F32, "acc_o"), mt, nh) for nh in range(2) for mt in range(M_TILES)]
         for g in range(F_GROUPS - TAIL_GROUPS):
-            for bank in banks:
-                down_pass(bank, g)
-            if g == 0:
-                flip((F_GROUPS - 1,))
-                quantise((F_GROUPS - 1,))
+            for out_bank in outs:
+                down_pass(out_bank, g)
+            if g == 1:
+                flip(N_PAIRS - 1)
+                quantise(N_PAIRS - 1)
         tail = range(F_GROUPS - TAIL_GROUPS, F_GROUPS)
         for i in range(2):
             for g in tail:
-                down_pass(banks[i], g)
-            store(banks[i], i == 0)
+                down_pass(outs[i], g)
+            store(outs[i], i == 0)
         for g in tail:
-            for bank in banks[2:]:
-                down_pass(bank, g)
-        store(banks[2], True)
-        store(banks[3], False)
-        store(banks[4], False)
+            for out_bank in outs[2:]:
+                down_pass(out_bank, g)
+        store(outs[2], True)
+        store(outs[3], False)

@@ -18,13 +18,13 @@ D_GROUPS = D // K_PASS
 F_GROUPS = F // K_PASS
 N_TILE = 512
 PAIR = 2 * K_PASS
-N_PAIRS = F // PAIR
+BLOCKS = ((0, 1), (2, 3))
+BLOCK = 2 * PAIR
 
 FLOPS = 2 * M * D * F * 3
 
-GATE_BATCHES = ((0, 1, "sync"), (1, 2, "sync"), (2, 3, "sync"), (3, 4, "gpsimd"))
-UP_BATCHES = ((0, 1, "sync"), (1, 4, "gpsimd"))
 TAIL_GROUPS = 2
+HEAD_GROUPS = 2
 
 
 def tile_mlp_kernel(
@@ -45,48 +45,31 @@ def tile_mlp_kernel(
 
         ident_f = keep.tile([P, P], F32)
         make_identity(nc, ident_f[:])
-        ident_b = keep.tile([P, P], BF16)
-        make_identity(nc, ident_b[:])
 
         warm_in = keep.tile([P, 8], F32)
         warm_out = keep.tile([P, 8], F32)
         nc.vector.memset(warm_in[:], 0.0)
         nc.scalar.activation(out=warm_out[:], in_=warm_in[:], func=silu)
 
-        def plane_tiles(batches, name):
-            return [
-                keep.tile([P, (hi - lo) * PAIR], U8, name="%s%d" % (name, lo), align_bytes=64)
-                for lo, hi, queue in batches
-            ]
-
-        gate_pl = plane_tiles(GATE_BATCHES, "gate_pl")
-        up_pl = plane_tiles(UP_BATCHES, "up_pl")
+        gate_pl = [keep.tile([P, BLOCK], U8, name="gate_pl%d" % b, align_bytes=64) for b in range(2)]
+        up_pl = keep.tile([P, F], U8, align_bytes=64)
         down_pl = [keep.tile([P, D], U8, name="down_pl%d" % a, align_bytes=64) for a in range(2)]
-        for pl in (up_pl[1], gate_pl[0], up_pl[0], gate_pl[3], gate_pl[1], gate_pl[2], down_pl[1], down_pl[0]):
+        for pl in (up_pl, gate_pl[0], gate_pl[1], down_pl[0], down_pl[1]):
             nc.vector.memset(pl[:].bitcast(I32), 0)
 
-        def load_planes(planes, scales, batch):
-            lo, hi, queue = batch
+        for q in range(4):
+            nc.gpsimd.dma_start(
+                out=up_pl[32 * q : 32 * q + 8, :].bitcast(F32),
+                in_=up_scales[:, 4 * q : 4 * q + 4, :].bitcast(F32),
+            )
+        ident_b = keep.tile([P, P], BF16)
+        make_identity(nc, ident_b[:])
+        for a in range(2):
             for q in range(4):
-                dst = planes[32 * q : 32 * q + 8, :]
-                src = scales[:, 4 * q : 4 * q + 4, lo * PAIR : hi * PAIR]
-                if queue == "sync":
-                    nc.sync.dma_start(out=dst.bitcast(I32), in_=src.bitcast(I32))
-                else:
-                    nc.gpsimd.dma_start(out=dst.bitcast(F32), in_=src.bitcast(F32))
-
-        def load_down_planes(a, queue):
-            for q in range(4):
-                dst = down_pl[a][32 * q : 32 * q + 16, :]
-                src = down_scales[4 * a : 4 * a + 4, 4 * q : 4 * q + 4, :]
-                if queue == "sync":
-                    nc.sync.dma_start(out=dst.bitcast(I32), in_=src.bitcast(I32))
-                else:
-                    nc.gpsimd.dma_start(out=dst.bitcast(F32), in_=src.bitcast(F32))
-
-        load_planes(up_pl[1], up_scales, UP_BATCHES[1])
-        load_planes(gate_pl[3], gate_scales, GATE_BATCHES[3])
-        load_down_planes(1, "gpsimd")
+                nc.gpsimd.dma_start(
+                    out=down_pl[a][32 * q : 32 * q + 16, :].bitcast(F32),
+                    in_=down_scales[4 * a : 4 * a + 4, 4 * q : 4 * q + 4, :].bitcast(F32),
+                )
 
         x_sb = []
         for mt in range(M_TILES):
@@ -107,19 +90,19 @@ def tile_mlp_kernel(
                 tiles.append(w_t)
             return tiles
 
-        gate_sb = []
-        up_sb = []
-        for j in range(N_PAIRS):
-            for i, batch in enumerate(GATE_BATCHES):
-                if batch[0] == j and batch[2] == "sync":
-                    load_planes(gate_pl[i], gate_scales, batch)
-            gate_sb.append(load_words(gate_words, j, "gate_sb"))
-            for i, batch in enumerate(UP_BATCHES):
-                if batch[0] == j and batch[2] == "sync":
-                    load_planes(up_pl[i], up_scales, batch)
-            up_sb.append(load_words(up_words, j, "up_sb"))
+        gate_sb = {}
+        up_sb = {}
+        for b, pairs in enumerate(BLOCKS):
+            for q in range(4):
+                nc.sync.dma_start(
+                    out=gate_pl[b][32 * q : 32 * q + 8, :].bitcast(I32),
+                    in_=gate_scales[:, 4 * q : 4 * q + 4, b * BLOCK : (b + 1) * BLOCK].bitcast(I32),
+                )
+            for j in pairs:
+                gate_sb[j] = load_words(gate_words, j, "gate_sb")
+            for j in pairs:
+                up_sb[j] = load_words(up_words, j, "up_sb")
 
-        load_down_planes(0, "sync")
         down_sb = {}
         for g in range(F_GROUPS - TAIL_GROUPS):
             d_t = keep.tile([P, D], U32, name="down_sb%d" % g, align_bytes=64)
@@ -145,11 +128,11 @@ def tile_mlp_kernel(
         x_banks = []
         for mt in range(M_TILES):
             xt = bank([P, D_GROUPS, 2, P], F32, "xt")
-            words = x_sb[mt][:].bitcast(F32)
+            x_words = x_sb[mt][:].bitcast(F32)
             for g in range(D_GROUPS):
                 for u in range(2):
                     nc.tensor.transpose(
-                        xt[:, g, u, :], words[:, 256 * g + u : 256 * (g + 1) : 2], ident_f[:]
+                        xt[:, g, u, :], x_words[:, 256 * g + u : 256 * (g + 1) : 2], ident_f[:]
                     )
             x_banks.append(xt)
         for mt in range(M_TILES):
@@ -173,11 +156,7 @@ def tile_mlp_kernel(
         def units(j):
             return [(2 * j + i, mt) for mt in range(M_TILES) for i in range(2)]
 
-        def project(words_sb, batches, tiles, j):
-            planes, at = None, 0
-            for i, (lo, hi, queue) in enumerate(batches):
-                if lo <= j < hi:
-                    planes, at = tiles[i], (j - lo) * PAIR
+        def project(words_sb, planes, at, j):
             accs = {}
             for unit in units(j):
                 accs[unit] = bank([P, K_PASS], F32, "acc")
@@ -195,23 +174,23 @@ def tile_mlp_kernel(
                     )
             return accs
 
+        acts = {}
+
         def gate_part(j):
-            accs = project(gate_sb, GATE_BATCHES, gate_pl, j)
-            acts = {}
+            accs = project(gate_sb, gate_pl[j // 2], (j % 2) * PAIR, j)
             for unit in units(j):
                 sg = work.tile([P, 4, P], F32, tag="sg", bufs=8, name="sg")
                 nc.scalar.activation(
                     out=sg[:], in_=accs[unit][:].rearrange("m (p t) -> m t p", t=4), func=silu
                 )
                 acts[unit] = sg
-            return acts
 
         hidden = {}
 
-        def up_part(j, acts):
-            accs = project(up_sb, UP_BATCHES, up_pl, j)
+        def up_part(j):
+            accs = project(up_sb, up_pl, j * PAIR, j)
             for unit in units(j):
-                h_sb = work.tile([P, 4, P], BF16, tag="h", bufs=12, name="h_sb")
+                h_sb = work.tile([P, 4, P], BF16, tag="h", bufs=8, name="h_sb")
                 nc.vector.tensor_tensor(
                     out=h_sb[:],
                     in0=acts[unit][:],
@@ -220,47 +199,45 @@ def tile_mlp_kernel(
                 )
                 hidden[unit] = h_sb
 
-        grouped = {}
-
-        def flip(j):
-            banks = []
-            for c in (2 * j, 2 * j + 1):
-                tr = bank([P, M_TILES, 4, P], BF16, "tr")
-                for mt in range(M_TILES):
-                    for t in range(4):
-                        nc.tensor.transpose(tr[:, mt, t, :], hidden[(c, mt)][:, t, :], ident_b[:])
-                banks.append(tr)
-            for i, c in enumerate((2 * j, 2 * j + 1)):
-                hg = work.tile([P, M_TILES, P, 4], BF16, tag="hg", bufs=4, name="hg", align_bytes=64)
-                src = banks[i][:].rearrange("p a t m -> p a m t")
-                if i == 0:
-                    nc.scalar.copy(out=hg[:], in_=src)
-                else:
-                    nc.vector.tensor_copy(out=hg[:], in_=src)
-                grouped[c] = hg
-
         h_codes = {}
         h_scales = {}
 
-        def quantise(j):
-            for c in (2 * j, 2 * j + 1):
-                hq = keep.tile([P, M_TILES, P], U32, name="hq%d" % c, align_bytes=64)
-                hs = keep.tile([P, M_TILES, P], U8, name="hs%d" % c, align_bytes=64)
-                nc.vector.quantize_mx(
-                    out=hq[:].rearrange("p a m -> p (a m)").bitcast(FP8X4),
-                    scales=hs[:].rearrange("p a m -> p (a m)"),
-                    in_=grouped[c][:].rearrange("p a m t -> p (a m t)"),
-                )
-                h_codes[c] = hq
-                h_scales[c] = hs
+        def flip(pairs):
+            banks = {}
+            for j in pairs:
+                for c in (2 * j, 2 * j + 1):
+                    banks[c] = bank([P, M_TILES, 4, P], BF16, "tr")
+                for c, mt in units(j):
+                    for t in range(4):
+                        nc.tensor.transpose(banks[c][:, mt, t, :], hidden[(c, mt)][:, t, :], ident_b[:])
+            for j in pairs:
+                grouped = {}
+                for i, c in enumerate((2 * j, 2 * j + 1)):
+                    hg = work.tile([P, M_TILES, P, 4], BF16, tag="hg", bufs=4, name="hg", align_bytes=64)
+                    src = banks[c][:].rearrange("p a t m -> p a m t")
+                    if i == 0:
+                        nc.scalar.copy(out=hg[:], in_=src)
+                    else:
+                        nc.vector.tensor_copy(out=hg[:], in_=src)
+                    grouped[c] = hg
+                for c in (2 * j, 2 * j + 1):
+                    hq = keep.tile([P, M_TILES, P], U32, name="hq%d" % c, align_bytes=64)
+                    hs = keep.tile([P, M_TILES, P], U8, name="hs%d" % c, align_bytes=64)
+                    nc.vector.quantize_mx(
+                        out=hq[:].rearrange("p a m -> p (a m)").bitcast(FP8X4),
+                        scales=hs[:].rearrange("p a m -> p (a m)"),
+                        in_=grouped[c][:].rearrange("p a m t -> p (a m t)"),
+                    )
+                    h_codes[c] = hq
+                    h_scales[c] = hs
 
-        for j in range(N_PAIRS):
-            acts = gate_part(j)
-            if j >= 1:
-                flip(j - 1)
-            up_part(j, acts)
-            if j >= 1:
-                quantise(j - 1)
+        for b, pairs in enumerate(BLOCKS):
+            for j in pairs:
+                gate_part(j)
+            for j in pairs:
+                up_part(j)
+            if b == 0:
+                flip(pairs)
 
         def down_pass(out_bank, g):
             acc, mt, nh = out_bank
@@ -290,9 +267,8 @@ def tile_mlp_kernel(
         for g in range(F_GROUPS - TAIL_GROUPS):
             for out_bank in outs:
                 down_pass(out_bank, g)
-            if g == 1:
-                flip(N_PAIRS - 1)
-                quantise(N_PAIRS - 1)
+            if g == HEAD_GROUPS - 1:
+                flip(BLOCKS[1])
         tail = range(F_GROUPS - TAIL_GROUPS, F_GROUPS)
         for i in range(2):
             for g in tail:

@@ -45,6 +45,8 @@ def tile_mlp_kernel(
 
         ident_f = keep.tile([P, P], F32)
         make_identity(nc, ident_f[:])
+        ident_b = keep.tile([P, P], BF16)
+        make_identity(nc, ident_b[:])
 
         warm_in = keep.tile([P, 8], F32)
         warm_out = keep.tile([P, 8], F32)
@@ -52,18 +54,17 @@ def tile_mlp_kernel(
         nc.scalar.activation(out=warm_out[:], in_=warm_in[:], func=silu)
 
         gate_pl = [keep.tile([P, BLOCK], U8, name="gate_pl%d" % b, align_bytes=64) for b in range(2)]
-        up_pl = keep.tile([P, F], U8, align_bytes=64)
+        up_pl = [keep.tile([P, BLOCK], U8, name="up_pl%d" % b, align_bytes=64) for b in range(2)]
         down_pl = [keep.tile([P, D], U8, name="down_pl%d" % a, align_bytes=64) for a in range(2)]
-        for pl in (up_pl, gate_pl[0], gate_pl[1], down_pl[0], down_pl[1]):
+        for pl in (gate_pl[0], up_pl[0], up_pl[1], gate_pl[1], down_pl[0], down_pl[1]):
             nc.vector.memset(pl[:].bitcast(I32), 0)
 
-        for q in range(4):
-            nc.gpsimd.dma_start(
-                out=up_pl[32 * q : 32 * q + 8, :].bitcast(F32),
-                in_=up_scales[:, 4 * q : 4 * q + 4, :].bitcast(F32),
-            )
-        ident_b = keep.tile([P, P], BF16)
-        make_identity(nc, ident_b[:])
+        for b in range(2):
+            for q in range(4):
+                nc.gpsimd.dma_start(
+                    out=up_pl[b][32 * q : 32 * q + 8, :].bitcast(F32),
+                    in_=up_scales[:, 4 * q : 4 * q + 4, b * BLOCK : (b + 1) * BLOCK].bitcast(F32),
+                )
         for a in range(2):
             for q in range(4):
                 nc.gpsimd.dma_start(
@@ -188,7 +189,7 @@ def tile_mlp_kernel(
         hidden = {}
 
         def up_part(j):
-            accs = project(up_sb, up_pl, j * PAIR, j)
+            accs = project(up_sb, up_pl[j // 2], (j % 2) * PAIR, j)
             for unit in units(j):
                 h_sb = work.tile([P, 4, P], BF16, tag="h", bufs=8, name="h_sb")
                 nc.vector.tensor_tensor(
@@ -202,34 +203,38 @@ def tile_mlp_kernel(
         h_codes = {}
         h_scales = {}
 
+        banks = {}
+        grouped = {}
+
         def flip(pairs):
-            banks = {}
             for j in pairs:
                 for c in (2 * j, 2 * j + 1):
                     banks[c] = bank([P, M_TILES, 4, P], BF16, "tr")
                 for c, mt in units(j):
                     for t in range(4):
                         nc.tensor.transpose(banks[c][:, mt, t, :], hidden[(c, mt)][:, t, :], ident_b[:])
-            for j in pairs:
-                grouped = {}
-                for i, c in enumerate((2 * j, 2 * j + 1)):
-                    hg = work.tile([P, M_TILES, P, 4], BF16, tag="hg", bufs=4, name="hg", align_bytes=64)
-                    src = banks[c][:].rearrange("p a t m -> p a m t")
-                    if i == 0:
-                        nc.scalar.copy(out=hg[:], in_=src)
-                    else:
-                        nc.vector.tensor_copy(out=hg[:], in_=src)
-                    grouped[c] = hg
-                for c in (2 * j, 2 * j + 1):
-                    hq = keep.tile([P, M_TILES, P], U32, name="hq%d" % c, align_bytes=64)
-                    hs = keep.tile([P, M_TILES, P], U8, name="hs%d" % c, align_bytes=64)
-                    nc.vector.quantize_mx(
-                        out=hq[:].rearrange("p a m -> p (a m)").bitcast(FP8X4),
-                        scales=hs[:].rearrange("p a m -> p (a m)"),
-                        in_=grouped[c][:].rearrange("p a m t -> p (a m t)"),
-                    )
-                    h_codes[c] = hq
-                    h_scales[c] = hs
+
+        def empty(j):
+            for i, c in enumerate((2 * j, 2 * j + 1)):
+                hg = work.tile([P, M_TILES, P, 4], BF16, tag="hg", bufs=4, name="hg", align_bytes=64)
+                src = banks[c][:].rearrange("p a t m -> p a m t")
+                if i == 0:
+                    nc.scalar.copy(out=hg[:], in_=src)
+                else:
+                    nc.vector.tensor_copy(out=hg[:], in_=src)
+                grouped[c] = hg
+
+        def quantise(j):
+            for c in (2 * j, 2 * j + 1):
+                hq = keep.tile([P, M_TILES, P], U32, name="hq%d" % c, align_bytes=64)
+                hs = keep.tile([P, M_TILES, P], U8, name="hs%d" % c, align_bytes=64)
+                nc.vector.quantize_mx(
+                    out=hq[:].rearrange("p a m -> p (a m)").bitcast(FP8X4),
+                    scales=hs[:].rearrange("p a m -> p (a m)"),
+                    in_=grouped[c][:].rearrange("p a m t -> p (a m t)"),
+                )
+                h_codes[c] = hq
+                h_scales[c] = hs
 
         for b, pairs in enumerate(BLOCKS):
             for j in pairs:
@@ -238,6 +243,10 @@ def tile_mlp_kernel(
                 up_part(j)
             if b == 0:
                 flip(pairs)
+                for j in pairs:
+                    empty(j)
+                for j in pairs:
+                    quantise(j)
 
         def down_pass(out_bank, g):
             acc, mt, nh = out_bank
@@ -269,6 +278,9 @@ def tile_mlp_kernel(
                 down_pass(out_bank, g)
             if g == HEAD_GROUPS - 1:
                 flip(BLOCKS[1])
+                for j in BLOCKS[1]:
+                    empty(j)
+                    quantise(j)
         tail = range(F_GROUPS - TAIL_GROUPS, F_GROUPS)
         for i in range(2):
             for g in tail:

from contextlib import ExitStack

import concourse.mybir as mybir
from concourse.masks import make_identity

FP8X4 = mybir.dt.float8_e4m3fn_x4
BF16 = mybir.dt.bfloat16
F32 = mybir.dt.float32
I32 = mybir.dt.int32
U32 = mybir.dt.uint32
U8 = mybir.dt.uint8

P = 128
M, D, F = 256, 1024, 4096
M_TILES = M // P
K_PASS = 512
D_GROUPS = D // K_PASS
F_GROUPS = F // K_PASS
N_TILE = 512
PAIR = 2 * K_PASS
BLOCKS = ((0, 1), (2, 3))
BLOCK = 2 * PAIR

FLOPS = 2 * M * D * F * 3

TAIL_GROUPS = 2
HEAD_GROUPS = 2


def tile_mlp_kernel(
    tc, x, gate_words, gate_scales, up_words, up_scales, down_words, down_scales, out
):
    nc = tc.nc
    silu = mybir.ActivationFunctionType.Silu
    mult = mybir.AluOpType.mult

    with ExitStack() as ctx:
        keep = ctx.enter_context(tc.tile_pool(name="keep", bufs=1))
        work = ctx.enter_context(tc.tile_pool(name="work", bufs=1))
        psum = ctx.enter_context(tc.psum_pool(name="psum", bufs=1))
        ctx.enter_context(tc.manual_schedule())

        def bank(shape, dtype, name):
            return psum.tile(shape, dtype, tag="bank", bufs=8, name=name)

        ident_f = keep.tile([P, P], F32)
        make_identity(nc, ident_f[:])
        ident_b = keep.tile([P, P], BF16)
        make_identity(nc, ident_b[:])

        warm_in = keep.tile([P, 8], F32)
        warm_out = keep.tile([P, 8], F32)
        nc.vector.memset(warm_in[:], 0.0)
        nc.scalar.activation(out=warm_out[:], in_=warm_in[:], func=silu)

        gate_pl = [keep.tile([P, BLOCK], U8, name="gate_pl%d" % b, align_bytes=64) for b in range(2)]
        up_pl = [keep.tile([P, BLOCK], U8, name="up_pl%d" % b, align_bytes=64) for b in range(2)]
        down_pl = [keep.tile([P, D], U8, name="down_pl%d" % a, align_bytes=64) for a in range(2)]
        for pl in (gate_pl[0], up_pl[0], up_pl[1], gate_pl[1], down_pl[0], down_pl[1]):
            nc.vector.memset(pl[:].bitcast(I32), 0)

        for b in range(2):
            for q in range(4):
                nc.gpsimd.dma_start(
                    out=up_pl[b][32 * q : 32 * q + 8, :].bitcast(F32),
                    in_=up_scales[:, 4 * q : 4 * q + 4, b * BLOCK : (b + 1) * BLOCK].bitcast(F32),
                )
        for a in range(2):
            for q in range(4):
                nc.gpsimd.dma_start(
                    out=down_pl[a][32 * q : 32 * q + 16, :].bitcast(F32),
                    in_=down_scales[4 * a : 4 * a + 4, 4 * q : 4 * q + 4, :].bitcast(F32),
                )

        x_sb = []
        for mt in range(M_TILES):
            x_t = keep.tile([P, D], BF16, name="x_sb%d" % mt)
            nc.sync.dma_start(out=x_t[:], in_=x[mt * P : (mt + 1) * P, :])
            x_sb.append(x_t)

        def load_words(words, j, name):
            tiles = []
            for g in range(D_GROUPS):
                w_t = keep.tile([P, PAIR], U32, name="%s%d_%d" % (name, j, g), align_bytes=64)
                nc.sync.dma_start(
                    out=w_t[:].bitcast(I32),
                    in_=words[g].rearrange("p n t -> p (n t)")[
                        :, 4 * PAIR * j : 4 * PAIR * (j + 1)
                    ].bitcast(I32),
                )
                tiles.append(w_t)
            return tiles

        gate_sb = {}
        up_sb = {}
        for b, pairs in enumerate(BLOCKS):
            for q in range(4):
                nc.sync.dma_start(
                    out=gate_pl[b][32 * q : 32 * q + 8, :].bitcast(I32),
                    in_=gate_scales[:, 4 * q : 4 * q + 4, b * BLOCK : (b + 1) * BLOCK].bitcast(I32),
                )
            for j in pairs:
                gate_sb[j] = load_words(gate_words, j, "gate_sb")
            for j in pairs:
                up_sb[j] = load_words(up_words, j, "up_sb")

        down_sb = {}
        for g in range(F_GROUPS - TAIL_GROUPS):
            d_t = keep.tile([P, D], U32, name="down_sb%d" % g, align_bytes=64)
            nc.sync.dma_start(
                out=d_t[:].bitcast(I32),
                in_=down_words[g].rearrange("p n t -> p (n t)").bitcast(I32),
            )
            for nh in range(2):
                down_sb[(g, nh)] = (d_t, nh * N_TILE)
        for nh in range(2):
            for g in range(F_GROUPS - TAIL_GROUPS, F_GROUPS):
                d_t = keep.tile([P, N_TILE], U32, name="down_sb%d_%d" % (g, nh), align_bytes=64)
                nc.sync.dma_start(
                    out=d_t[:].bitcast(I32),
                    in_=down_words[g].rearrange("p n t -> p (n t)")[
                        :, 4 * N_TILE * nh : 4 * N_TILE * (nh + 1)
                    ].bitcast(I32),
                )
                down_sb[(g, nh)] = (d_t, 0)

        x_codes = []
        x_scales = []
        x_banks = []
        for mt in range(M_TILES):
            xt = bank([P, D_GROUPS, 2, P], F32, "xt")
            x_words = x_sb[mt][:].bitcast(F32)
            for g in range(D_GROUPS):
                for u in range(2):
                    nc.tensor.transpose(
                        xt[:, g, u, :], x_words[:, 256 * g + u : 256 * (g + 1) : 2], ident_f[:]
                    )
            x_banks.append(xt)
        for mt in range(M_TILES):
            xg = keep.tile([P, D_GROUPS * P * 4], BF16, name="xg%d" % mt, align_bytes=64)
            dst = xg[:].bitcast(F32).rearrange("p (g m u) -> p g m u", g=D_GROUPS, u=2)
            src = x_banks[mt][:].rearrange("p g u m -> p g m u")
            if mt == 0:
                nc.vector.tensor_copy(out=dst, in_=src)
            else:
                nc.scalar.copy(out=dst, in_=src)
            xq = keep.tile([P, D_GROUPS, P], U32, name="xq%d" % mt, align_bytes=64)
            xs = keep.tile([P, D_GROUPS, P], U8, name="xs%d" % mt, align_bytes=64)
            nc.vector.quantize_mx(
                out=xq[:].rearrange("p g m -> p (g m)").bitcast(FP8X4),
                scales=xs[:].rearrange("p g m -> p (g m)"),
                in_=xg[:],
            )
            x_codes.append(xq)
            x_scales.append(xs)

        def units(j):
            return [(2 * j + i, mt) for mt in range(M_TILES) for i in range(2)]

        def project(words_sb, planes, at, j):
            accs = {}
            for unit in units(j):
                accs[unit] = bank([P, K_PASS], F32, "acc")
            for g in range(D_GROUPS):
                for c, mt in units(j):
                    col = (c % 2) * K_PASS
                    nc.tensor.matmul_mx(
                        out=accs[(c, mt)][:],
                        lhsT=x_codes[mt][:, g, :].bitcast(FP8X4),
                        lhsT_scale=x_scales[mt][:, g, :],
                        rhs=words_sb[j][g][:, col : col + K_PASS].bitcast(FP8X4),
                        rhs_scale=planes[4 * g : P, at + col : at + col + K_PASS],
                        start=(g == 0),
                        stop=(g == D_GROUPS - 1),
                    )
            return accs

        acts = {}

        def gate_part(j):
            accs = project(gate_sb, gate_pl[j // 2], (j % 2) * PAIR, j)
            for unit in units(j):
                sg = work.tile([P, 4, P], F32, tag="sg", bufs=8, name="sg")
                nc.scalar.activation(
                    out=sg[:], in_=accs[unit][:].rearrange("m (p t) -> m t p", t=4), func=silu
                )
                acts[unit] = sg

        hidden = {}

        def up_part(j):
            accs = project(up_sb, up_pl[j // 2], (j % 2) * PAIR, j)
            for unit in units(j):
                h_sb = work.tile([P, 4, P], BF16, tag="h", bufs=8, name="h_sb")
                nc.vector.tensor_tensor(
                    out=h_sb[:],
                    in0=acts[unit][:],
                    in1=accs[unit][:].rearrange("m (p t) -> m t p", t=4),
                    op=mult,
                )
                hidden[unit] = h_sb

        h_codes = {}
        h_scales = {}

        banks = {}
        grouped = {}

        def flip(pairs):
            for j in pairs:
                for c in (2 * j, 2 * j + 1):
                    banks[c] = bank([P, M_TILES, 4, P], BF16, "tr")
                for c, mt in units(j):
                    for t in range(4):
                        nc.tensor.transpose(banks[c][:, mt, t, :], hidden[(c, mt)][:, t, :], ident_b[:])

        def empty(j):
            for i, c in enumerate((2 * j, 2 * j + 1)):
                hg = work.tile([P, M_TILES, P, 4], BF16, tag="hg", bufs=4, name="hg", align_bytes=64)
                src = banks[c][:].rearrange("p a t m -> p a m t")
                if i == 0:
                    nc.scalar.copy(out=hg[:], in_=src)
                else:
                    nc.vector.tensor_copy(out=hg[:], in_=src)
                grouped[c] = hg

        def quantise(j):
            for c in (2 * j, 2 * j + 1):
                hq = keep.tile([P, M_TILES, P], U32, name="hq%d" % c, align_bytes=64)
                hs = keep.tile([P, M_TILES, P], U8, name="hs%d" % c, align_bytes=64)
                nc.vector.quantize_mx(
                    out=hq[:].rearrange("p a m -> p (a m)").bitcast(FP8X4),
                    scales=hs[:].rearrange("p a m -> p (a m)"),
                    in_=grouped[c][:].rearrange("p a m t -> p (a m t)"),
                )
                h_codes[c] = hq
                h_scales[c] = hs

        for b, pairs in enumerate(BLOCKS):
            for j in pairs:
                gate_part(j)
            for j in pairs:
                up_part(j)
            if b == 0:
                flip(pairs)
                for j in pairs:
                    empty(j)
                for j in pairs:
                    quantise(j)

        def down_pass(out_bank, g):
            acc, mt, nh = out_bank
            d_t, at = down_sb[(g, nh)]
            nc.tensor.matmul_mx(
                out=acc[:],
                lhsT=h_codes[g][:, mt, :].bitcast(FP8X4),
                lhsT_scale=h_scales[g][:, mt, :],
                rhs=d_t[:, at : at + N_TILE].bitcast(FP8X4),
                rhs_scale=down_pl[g // 4][4 * (g % 4) : P, nh * N_TILE : (nh + 1) * N_TILE],
                start=(g == 0),
                stop=(g == F_GROUPS - 1),
            )

        def store(out_bank, on_scalar):
            acc, mt, nh = out_bank
            o_sb = work.tile([P, N_TILE], F32, tag="o", bufs=4, name="o_sb")
            if on_scalar:
                nc.scalar.copy(out=o_sb[:], in_=acc[:])
            else:
                nc.vector.tensor_copy(out=o_sb[:], in_=acc[:])
            nc.sync.dma_start(
                out=out[mt * P : (mt + 1) * P, nh * N_TILE : (nh + 1) * N_TILE], in_=o_sb[:]
            )

        outs = [(bank([P, N_TILE], F32, "acc_o"), mt, nh) for nh in range(2) for mt in range(M_TILES)]
        for g in range(F_GROUPS - TAIL_GROUPS):
            for out_bank in outs:
                down_pass(out_bank, g)
            if g == HEAD_GROUPS - 1:
                flip(BLOCKS[1])
                for j in BLOCKS[1]:
                    empty(j)
                    quantise(j)
        tail = range(F_GROUPS - TAIL_GROUPS, F_GROUPS)
        for i in range(2):
            for g in tail:
                down_pass(outs[i], g)
            store(outs[i], i == 0)
        for g in tail:
            for out_bank in outs[2:]:
                down_pass(out_bank, g)
        store(outs[2], True)
        store(outs[3], False)
